import numpy as np
import ml_dtypes


def mxq(x, axis, fmt="e4m3"):
    dtype, down = {"e4m3": (ml_dtypes.float8_e4m3fn, 7), "e5m2": (ml_dtypes.float8_e5m2, 14)}[fmt]
    v = np.moveaxis(np.asarray(x, np.float32).astype(ml_dtypes.bfloat16).astype(np.float64), axis, -1)
    blocks = v.reshape(v.shape[:-1] + (-1, 32))
    amax = np.abs(blocks).max(-1, keepdims=True)
    byte = np.maximum(np.where(amax > 0, np.frexp(amax)[1] - 1 + 127, 0) - down, 1)
    scale = np.exp2(byte - 127.0)
    codes = (blocks / scale).astype(np.float32).astype(dtype).astype(np.float64)
    return np.moveaxis((codes * scale).reshape(v.shape), -1, axis)


WIDE = False


def mx_kscale(k):
    if not WIDE:
        return np.ones(k)
    levels = np.array([10, -10, 5, -5, 0])
    if k % 512:
        return np.exp2(np.random.permutation(np.resize(levels, k // 32))).repeat(32)
    a = np.empty((k // 512, 16))
    for p in range(k // 512):
        a[p, :8] = np.random.permutation(np.resize(levels, 8))
        for g in range(8):
            far = levels[np.abs(levels - a[p, g]) >= 10]
            a[p, g + 8] = far[np.random.randint(len(far))]
    return np.exp2(a.ravel()).repeat(32)


BF16 = ml_dtypes.bfloat16


def bf(x):
    return np.asarray(x, np.float32).astype(BF16)


def f64(x):
    return np.asarray(x).astype(np.float64)


B, I, H, ORDER = 8192, 512, 256, 2
OH = ORDER * H


def sigmoid(v):
    return 1.0 / (1.0 + np.exp(-v))


def setup_inputs():
    s, t = mx_kscale(I), mx_kscale(OH)
    return {"x": bf(np.random.standard_normal((B, I)) * s),
            "me_output": bf(np.random.standard_normal((B, OH)) * t),
            "W_memi": bf(np.random.standard_normal((I, OH)) * 0.7 / np.sqrt(I) / s[:, None]),
            "W_memh": bf(np.random.standard_normal((OH, OH)) * 0.7 / np.sqrt(OH) / t[:, None]),
            "W_memt": bf(np.random.standard_normal((OH, H)) * 1.0 / np.sqrt(OH) / t[:, None]),
            "mem_bias": bf(np.random.standard_normal(OH) * 0.3)}


def reference(x, me_output, W_memi, W_memh, W_memt, mem_bias):
    me = f64(me_output)
    mg = ((mxq(f64(x), 1, "e4m3") @ mxq(f64(W_memi), 0, "e4m3"))
          + (mxq(me, 1, "e4m3") @ mxq(f64(W_memh), 0, "e4m3"))
          + f64(mem_bias))
    gated = sigmoid(mg) * me
    return mxq(gated, 1, "e4m3") @ mxq(f64(W_memt), 0, "e4m3")

@@ -1,0 +1,264 @@
+from contextlib import ExitStack
+
+import concourse.mybir as mybir
+from concourse.masks import make_identity
+
+F32 = mybir.dt.float32
+BF16 = mybir.dt.bfloat16
+U32 = mybir.dt.uint32
+U8 = mybir.dt.uint8
+FP8X4 = mybir.dt.float8_e4m3fn_x4
+ACT = mybir.ActivationFunctionType
+ALU = mybir.AluOpType
+
+B, I, OH, H = 8192, 512, 512, 256
+FLOPS = 2 * B * (I * OH + OH * OH + OH * H)
+
+P = 128
+ROW_TILES = [2, 2] + [4] * 14 + [2, 2]
+NB = len(ROW_TILES)
+ROW0 = [P * sum(ROW_TILES[:j]) for j in range(NB)]
+assert P * sum(ROW_TILES) == B
+LOOKAHEAD = 6
+NAT_BUFS = 6
+S2_LAG = 1
+
+
+def vector_exits(j):
+    if j < 2:
+        return 0
+    return 2 if ROW_TILES[j] == 4 and j % 3 == 1 else 1
+
+
+def gpsimd_cols(j):
+    if ROW_TILES[j] != 4 or j + 2 >= NB:
+        return 0
+    return 96 if vector_exits(j + 2) == 2 else 48
+
+
+def tile_lstmcell_pa_t_kernel(tc, x, me_output, W_memi, W_memh, W_memt, mem_bias, out):
+    nc = tc.nc
+    with ExitStack() as ctx:
+        consts = ctx.enter_context(tc.tile_pool(name="consts", bufs=1))
+        nat = ctx.enter_context(tc.tile_pool(name="nat", bufs=NAT_BUFS))
+        work = ctx.enter_context(tc.tile_pool(name="work", bufs=2))
+        psum = ctx.enter_context(tc.psum_pool(name="psum", bufs=1))
+        ctx.enter_context(tc.manual_schedule())
+
+        counter = [0]
+
+        def new_bank():
+            n = counter[0]
+            counter[0] = n + 1
+            return psum.tile([P, 512], F32, name="ps%d" % n, tag="bank%d" % (n % 8))
+
+        st = {}
+
+        warm = consts.tile([P, 1], F32, name="warm")
+        nc.vector.memset(warm[:], 0.0)
+        nc.scalar.activation(out=warm[:], in_=warm[:], func=ACT.Sigmoid)
+
+        ident = consts.tile([P, P], F32, name="ident")
+        make_identity(nc, ident[:])
+
+        bias_raw = consts.tile([P, 4], BF16, name="bias_raw")
+        with nc.allow_non_contiguous_dma(reason="512 bias values, four to a partition"):
+            nc.scalar.dma_start(out=bias_raw[:], in_=mem_bias.rearrange("(p t) -> p t", t=4))
+
+        def load_w(w, cols, nm):
+            raw = consts.tile([P, 4 * cols], BF16, name=nm + "_raw")
+            nc.sync.dma_start(out=raw[:], in_=w.rearrange("(p j) c -> p (j c)", j=4))
+            return raw
+
+        def load(j):
+            nr = ROW_TILES[j]
+            rows = slice(ROW0[j], ROW0[j] + nr * P)
+            xn = nat.tile([P, nr * I], BF16, name="xn%d" % j, tag="xn")
+            nc.sync.dma_start(out=xn[:], in_=x[rows, :].rearrange("(p r) k -> p (r k)", r=nr))
+            en = nat.tile([P, nr * OH], BF16, name="en%d" % j, tag="en")
+            nc.sync.dma_start(out=en[:], in_=me_output[rows, :].rearrange("(p r) k -> p (r k)", r=nr))
+            st[("xn", j)] = xn
+            st[("en", j)] = en
+
+        wi_raw = load_w(W_memi, OH, "wi")
+        wh_raw = load_w(W_memh, OH, "wh")
+        load(0)
+        load(1)
+        wt_raw = load_w(W_memt, H, "wt")
+        load(2)
+        load(3)
+        loaded = [4]
+
+        def regroup_gate_w(raw, nm, engines):
+            grp = consts.tile([P, 4 * OH], BF16, name=nm + "_grp", align_bytes=64)
+            src = raw[:].rearrange("p (t q m) -> p m q t", t=4, m=4)
+            for m in range(4):
+                dst = grp[:, m * 512:(m + 1) * 512].rearrange("p (q t) -> p q t", t=4)
+                if engines[m] == "v":
+                    nc.vector.tensor_copy(out=dst, in_=src[:, m])
+                else:
+                    nc.scalar.copy(out=dst, in_=src[:, m])
+            return grp
+
+        def quant_w(grp, cols, nm):
+            codes = consts.tile([P, cols], U32, name=nm + "_codes", align_bytes=64)
+            scales = consts.tile([P, cols], U8, name=nm + "_scales", align_bytes=64)
+            nc.vector.quantize_mx(out=codes[:].bitcast(FP8X4), scales=scales[:], in_=grp[:])
+            return codes, scales
+
+        wi_grp = regroup_gate_w(wi_raw, "wi", "vvvs")
+        wic, wis = quant_w(wi_grp, OH, "wi")
+        wh_grp = regroup_gate_w(wh_raw, "wh", "ssvv")
+        whc, whs = quant_w(wh_grp, OH, "wh")
+        bias_f = consts.tile([P, 4], F32, name="bias_f")
+        nc.vector.tensor_copy(out=bias_f[:], in_=bias_raw[:])
+
+        def prep_wt():
+            grp = consts.tile([P, 4 * H], BF16, name="wt_grp", align_bytes=64)
+            nc.vector.tensor_copy(
+                out=grp[:].rearrange("p (h t) -> p h t", t=4),
+                in_=wt_raw[:].rearrange("p (t h) -> p h t", t=4),
+            )
+            st["wt_grp"] = grp
+
+        def quant_wt():
+            st["wt"] = quant_w(st["wt_grp"], H, "wt")
+
+        def transposes(j):
+            for key in ("xn", "en"):
+                words = st[(key, j)][:].bitcast(F32)
+                for h in range(ROW_TILES[j] // 2):
+                    bank = new_bank()
+                    for rr in range(2):
+                        for u in range(2):
+                            c0 = (2 * h + rr) * 256 + u
+                            nc.tensor.transpose(
+                                bank[:, u * 256 + rr * P:u * 256 + (rr + 1) * P],
+                                words[:, c0:c0 + 255:2],
+                                ident[:],
+                            )
+                    st[("T", key, j, h)] = bank
+
+        def exits(j):
+            nr = ROW_TILES[j]
+            gx = work.tile([P, nr * 512], BF16, name="gx%d" % j, tag="gx", align_bytes=64)
+            ge = work.tile([P, nr * 512], BF16, name="ge%d" % j, tag="ge", bufs=3, align_bytes=64)
+            st[("gx", j)] = gx
+            st[("ge", j)] = ge
+            plan = [("xn", gx, h) for h in range(nr // 2)] + [("en", ge, h) for h in range(nr // 2)]
+            n_vec = vector_exits(j)
+            for i, (key, dst, h) in enumerate(plan):
+                src = st[("T", key, j, h)][:].rearrange("q (u c) -> q c u", u=2)
+                d = dst[:].bitcast(F32)[:, h * 512:(h + 1) * 512].rearrange("q (c u) -> q c u", u=2)
+                if i >= len(plan) - n_vec:
+                    nc.vector.tensor_copy(out=d, in_=src)
+                else:
+                    nc.scalar.copy(out=d, in_=src)
+
+        def quant(src, nm, j, bufs):
+            cols = ROW_TILES[j] * P
+            codes = work.tile([P, cols], U32, name="%sc%d" % (nm, j), tag=nm + "c", bufs=bufs, align_bytes=64)
+            scales = work.tile([P, cols], U8, name="%ss%d" % (nm, j), tag=nm + "s", bufs=bufs, align_bytes=64)
+            nc.vector.quantize_mx(out=codes[:].bitcast(FP8X4), scales=scales[:], in_=src[:])
+            st[(nm, j)] = (codes, scales)
+
+        def stage1(j):
+            n = ROW_TILES[j] * P
+            per_bank = 512 // n
+            xc, xs = st[("x", j)]
+            ec, es = st[("e", j)]
+            bank = None
+            for m in range(4):
+                cols = slice(m * P, (m + 1) * P)
+                if m % per_bank == 0:
+                    bank = new_bank()
+                acc = bank[:, (m % per_bank) * n:(m % per_bank + 1) * n]
+                nc.tensor.matmul_mx(
+                    out=acc, lhsT=wic[:, cols].bitcast(FP8X4), lhsT_scale=wis[:, cols],
+                    rhs=xc[:].bitcast(FP8X4), rhs_scale=xs[:], start=True, stop=False,
+                )
+                nc.tensor.matmul_mx(
+                    out=acc, lhsT=whc[:, cols].bitcast(FP8X4), lhsT_scale=whs[:, cols],
+                    rhs=ec[:].bitcast(FP8X4), rhs_scale=es[:], start=False, stop=True,
+                )
+                st[("M", j, m)] = acc
+
+        def sigmoid(j):
+            n = ROW_TILES[j] * P
+            sig = work.tile([P, 4 * n], F32, name="sig%d" % j, tag="sig")
+            for m in range(4):
+                nc.scalar.activation(
+                    out=sig[:, m * n:(m + 1) * n], in_=st[("M", j, m)],
+                    func=ACT.Sigmoid, bias=bias_f[:, m:m + 1], scale=1.0,
+                )
+            st[("sig", j)] = sig
+
+        def mult(j):
+            n = ROW_TILES[j] * P
+            gg = work.tile([P, 4 * n], BF16, name="gg%d" % j, tag="gg", align_bytes=64)
+            nv = n - gpsimd_cols(j)
+            planes = st[("sig", j)][:].rearrange("p (t c) -> p t c", t=4)
+            ge = st[("ge", j)]
+            nc.vector.tensor_tensor(
+                out=gg[:, :4 * nv].rearrange("p (c i t) -> p c t i", i=4, t=4),
+                in0=planes[:, :, :nv].rearrange("p t (c i) -> p c t i", i=4),
+                in1=ge[:, :4 * nv].rearrange("p (c i t) -> p c t i", i=4, t=4),
+                op=ALU.mult,
+            )
+            if nv < n:
+                nc.gpsimd.tensor_tensor(
+                    out=gg[:, 4 * nv:].rearrange("p (c t) -> p c t", t=4),
+                    in0=planes[:, :, nv:].rearrange("p t c -> p c t"),
+                    in1=ge[:, 4 * nv:].rearrange("p (c t) -> p c t", t=4),
+                    op=ALU.mult,
+                )
+            st[("gg", j)] = gg
+
+        def stage2(j):
+            gc, gs = st[("g", j)]
+            wtc, wts = st["wt"]
+            for h in range(ROW_TILES[j] // 2):
+                bank = new_bank()
+                for rr in range(2):
+                    cols = slice((2 * h + rr) * P, (2 * h + rr + 1) * P)
+                    nc.tensor.matmul_mx(
+                        out=bank[:, rr * H:(rr + 1) * H],
+                        lhsT=gc[:, cols].bitcast(FP8X4), lhsT_scale=gs[:, cols],
+                        rhs=wtc[:].bitcast(FP8X4), rhs_scale=wts[:], start=True, stop=True,
+                    )
+                st[("O", j, h)] = bank
+
+        def oexit_store(j):
+            nr = ROW_TILES[j]
+            osb = work.tile([P, nr * H], F32, name="osb%d" % j, tag="osb", bufs=3)
+            for h in range(nr // 2):
+                nc.scalar.copy(out=osb[:, h * 512:(h + 1) * 512], in_=st[("O", j, h)][:])
+            nc.sync.dma_start(
+                out=out[ROW0[j]:ROW0[j] + nr * P, :].rearrange("(p r) h -> p (r h)", r=nr), in_=osb[:]
+            )
+
+        for s in range(-2, NB + S2_LAG):
+            while loaded[0] < NB and loaded[0] <= s + LOOKAHEAD:
+                load(loaded[0])
+                loaded[0] += 1
+            if s + 2 < NB:
+                transposes(s + 2)
+            if 0 <= s < NB:
+                mult(s)
+            if s + 2 < NB:
+                exits(s + 2)
+            if s == 0:
+                quant_wt()
+            if 0 <= s + 1 < NB:
+                stage1(s + 1)
+                sigmoid(s + 1)
+            if s + 2 < NB:
+                quant(st[("gx", s + 2)], "x", s + 2, 2)
+                quant(st[("ge", s + 2)], "e", s + 2, 2)
+            if 0 <= s < NB:
+                quant(st[("gg", s)], "g", s, 2 + S2_LAG)
+            if s == -1:
+                prep_wt()
+            if 0 <= s - S2_LAG < NB:
+                stage2(s - S2_LAG)
+                oexit_store(s - S2_LAG)

@@ -36,6 +36,10 @@ def gpsimd_cols(j):
     return 96 if vector_exits(j + 2) == 2 else 48
 
 
+def reorder_plan(j):
+    return [("xn", 0, 3)] if ROW_TILES[j] == 4 and j > 2 else []
+
+
 def tile_lstmcell_pa_t_kernel(tc, x, me_output, W_memi, W_memh, W_memt, mem_bias, out):
     nc = tc.nc
     with ExitStack() as ctx:
@@ -124,6 +128,17 @@ def tile_lstmcell_pa_t_kernel(tc, x, me_output, W_memi, W_memh, W_memt, mem_bias
         def quant_wt():
             st["wt"] = quant_w(st["wt_grp"], H, "wt")
 
+        def reorder(j):
+            for key, r0, m in reorder_plan(j):
+                dst = work.tile([P, m * 256], F32, name="%sw%d" % (key, j), tag=key + "w")
+                nc.vector.tensor_copy(
+                    out=dst[:].rearrange("p (r u q) -> p r u q", u=2, r=m),
+                    in_=st[(key, j)][:].bitcast(F32)[:, r0 * 256:(r0 + m) * 256].rearrange("p (r q u) -> p r u q", u=2, r=m),
+                )
+                for r in range(m):
+                    for u in range(2):
+                        st[("W", key, j, r0 + r, u)] = dst[:, (2 * r + u) * P:(2 * r + u + 1) * P]
+
         def transposes(j):
             for key in ("xn", "en"):
                 words = st[(key, j)][:].bitcast(F32)
@@ -132,11 +147,10 @@ def tile_lstmcell_pa_t_kernel(tc, x, me_output, W_memi, W_memh, W_memt, mem_bias
                     for rr in range(2):
                         for u in range(2):
                             c0 = (2 * h + rr) * 256 + u
-                            nc.tensor.transpose(
-                                bank[:, u * 256 + rr * P:u * 256 + (rr + 1) * P],
-                                words[:, c0:c0 + 255:2],
-                                ident[:],
-                            )
+                            src = st.get(("W", key, j, 2 * h + rr, u))
+                            if src is None:
+                                src = words[:, c0:c0 + 255:2]
+                            nc.tensor.transpose(bank[:, u * 256 + rr * P:u * 256 + (rr + 1) * P], src, ident[:])
                     st[("T", key, j, h)] = bank
 
         def exits(j):
@@ -243,6 +257,8 @@ def tile_lstmcell_pa_t_kernel(tc, x, me_output, W_memi, W_memh, W_memt, mem_bias
                 loaded[0] += 1
             if s + 2 < NB:
                 transposes(s + 2)
+            if 0 <= s + 3 < NB:
+                reorder(s + 3)
             if 0 <= s < NB:
                 mult(s)
             if s + 2 < NB:

@@ -37,7 +37,7 @@ def gpsimd_cols(j):
 
 
 def reorder_plan(j):
-    return [("xn", 0, 3)] if ROW_TILES[j] == 4 and j > 2 else []
+    return [("xn", 0, 2)] if ROW_TILES[j] == 4 and j > 2 else []
 
 
 def tile_lstmcell_pa_t_kernel(tc, x, me_output, W_memi, W_memh, W_memt, mem_bias, out):
@@ -132,8 +132,8 @@ def tile_lstmcell_pa_t_kernel(tc, x, me_output, W_memi, W_memh, W_memt, mem_bias
             for key, r0, m in reorder_plan(j):
                 dst = work.tile([P, m * 256], F32, name="%sw%d" % (key, j), tag=key + "w")
                 nc.vector.tensor_copy(
-                    out=dst[:].rearrange("p (r u q) -> p r u q", u=2, r=m),
-                    in_=st[(key, j)][:].bitcast(F32)[:, r0 * 256:(r0 + m) * 256].rearrange("p (r q u) -> p r u q", u=2, r=m),
+                    out=dst[:].rearrange("p (r u q) -> p u r q", u=2, r=m),
+                    in_=st[(key, j)][:].bitcast(F32)[:, r0 * 256:(r0 + m) * 256].rearrange("p (r q u) -> p u r q", u=2, r=m),
                 )
                 for r in range(m):
                     for u in range(2):

@@ -22,22 +22,29 @@ assert P * sum(ROW_TILES) == B
 LOOKAHEAD = 6
 NAT_BUFS = 6
 S2_LAG = 1
-
-
-def vector_exits(j):
-    if j < 2:
-        return 0
-    return 2 if ROW_TILES[j] == 4 and j % 3 == 1 else 1
-
-
-def gpsimd_cols(j):
-    if ROW_TILES[j] != 4 or j + 2 >= NB:
-        return 0
-    return 96 if vector_exits(j + 2) == 2 else 48
+RING_BANKS = 8
+HELD_BANKS = 0
+REORDER_LEAD = 3
 
 
 def reorder_plan(j):
-    return [("xn", 0, 2)] if ROW_TILES[j] == 4 and j > 2 else []
+    nr = ROW_TILES[j]
+    return [("xn", 0, 1)] if nr == 4 and j >= 4 else []
+
+
+def vector_exits(j):
+    nr = ROW_TILES[j]
+    return (0 if j < 2 else 1 if nr < 4 else 2 if j % 3 == 1 else 1)
+
+
+def psum_cols(j):
+    nr = ROW_TILES[j]
+    return 0
+
+
+def gpsimd_cols(j):
+    nr = ROW_TILES[j]
+    return (48 * vector_exits(j + 2) if nr == 4 and j + 2 < NB else 0)
 
 
 def tile_lstmcell_pa_t_kernel(tc, x, me_output, W_memi, W_memh, W_memt, mem_bias, out):
@@ -54,7 +61,7 @@ def tile_lstmcell_pa_t_kernel(tc, x, me_output, W_memi, W_memh, W_memt, mem_bias
         def new_bank():
             n = counter[0]
             counter[0] = n + 1
-            return psum.tile([P, 512], F32, name="ps%d" % n, tag="bank%d" % (n % 8))
+            return psum.tile([P, 512], F32, name="ps%d" % n, tag="bank%d" % (n % RING_BANKS))
 
         st = {}
 
@@ -110,12 +117,14 @@ def tile_lstmcell_pa_t_kernel(tc, x, me_output, W_memi, W_memh, W_memt, mem_bias
             nc.vector.quantize_mx(out=codes[:].bitcast(FP8X4), scales=scales[:], in_=grp[:])
             return codes, scales
 
-        wi_grp = regroup_gate_w(wi_raw, "wi", "vvvs")
-        wic, wis = quant_w(wi_grp, OH, "wi")
-        wh_grp = regroup_gate_w(wh_raw, "wh", "ssvv")
-        whc, whs = quant_w(wh_grp, OH, "wh")
         bias_f = consts.tile([P, 4], F32, name="bias_f")
-        nc.vector.tensor_copy(out=bias_f[:], in_=bias_raw[:])
+
+        def prep_gate():
+            wi_grp = regroup_gate_w(wi_raw, "wi", "vvvs")
+            st["wi"] = quant_w(wi_grp, OH, "wi")
+            wh_grp = regroup_gate_w(wh_raw, "wh", "ssvv")
+            st["wh"] = quant_w(wh_grp, OH, "wh")
+            nc.vector.tensor_copy(out=bias_f[:], in_=bias_raw[:])
 
         def prep_wt():
             grp = consts.tile([P, 4 * H], BF16, name="wt_grp", align_bytes=64)
@@ -139,31 +148,39 @@ def tile_lstmcell_pa_t_kernel(tc, x, me_output, W_memi, W_memh, W_memt, mem_bias
                     for u in range(2):
                         st[("W", key, j, r0 + r, u)] = dst[:, (2 * r + u) * P:(2 * r + u + 1) * P]
 
+        def halves(j):
+            return [(h, min(2, ROW_TILES[j] - 2 * h)) for h in range((ROW_TILES[j] + 1) // 2)]
+
         def transposes(j):
             for key in ("xn", "en"):
                 words = st[(key, j)][:].bitcast(F32)
-                for h in range(ROW_TILES[j] // 2):
-                    bank = new_bank()
-                    for rr in range(2):
+                for h, m in halves(j):
+                    if HELD_BANKS and key == "en" and h == len(halves(j)) - 1:
+                        bank = psum.tile([P, 512], F32, name="held%d" % j, tag="held", bufs=HELD_BANKS)
+                    else:
+                        bank = new_bank()
+                    for rr in range(m):
                         for u in range(2):
                             c0 = (2 * h + rr) * 256 + u
                             src = st.get(("W", key, j, 2 * h + rr, u))
                             if src is None:
                                 src = words[:, c0:c0 + 255:2]
-                            nc.tensor.transpose(bank[:, u * 256 + rr * P:u * 256 + (rr + 1) * P], src, ident[:])
+                            nc.tensor.transpose(bank[:, (u * m + rr) * P:(u * m + rr + 1) * P], src, ident[:])
                     st[("T", key, j, h)] = bank
 
-        def exits(j):
+        def exit_tiles(j):
             nr = ROW_TILES[j]
-            gx = work.tile([P, nr * 512], BF16, name="gx%d" % j, tag="gx", align_bytes=64)
-            ge = work.tile([P, nr * 512], BF16, name="ge%d" % j, tag="ge", bufs=3, align_bytes=64)
-            st[("gx", j)] = gx
-            st[("ge", j)] = ge
-            plan = [("xn", gx, h) for h in range(nr // 2)] + [("en", ge, h) for h in range(nr // 2)]
+            st[("gx", j)] = work.tile([P, nr * 512], BF16, name="gx%d" % j, tag="gx", bufs=2, align_bytes=64)
+            st[("ge", j)] = work.tile([P, nr * 512], BF16, name="ge%d" % j, tag="ge", bufs=3, align_bytes=64)
+
+        def exits(j):
+            exit_tiles(j)
+            gx, ge = st[("gx", j)], st[("ge", j)]
+            plan = [("xn", gx, h, m) for h, m in halves(j)] + [("en", ge, h, m) for h, m in halves(j)]
             n_vec = vector_exits(j)
-            for i, (key, dst, h) in enumerate(plan):
-                src = st[("T", key, j, h)][:].rearrange("q (u c) -> q c u", u=2)
-                d = dst[:].bitcast(F32)[:, h * 512:(h + 1) * 512].rearrange("q (c u) -> q c u", u=2)
+            for i, (key, dst, h, m) in enumerate(plan):
+                src = st[("T", key, j, h)][:, :m * 256].rearrange("q (u c) -> q c u", u=2)
+                d = dst[:].bitcast(F32)[:, h * 512:h * 512 + m * 256].rearrange("q (c u) -> q c u", u=2)
                 if i >= len(plan) - n_vec:
                     nc.vector.tensor_copy(out=d, in_=src)
                 else:
@@ -173,14 +190,22 @@ def tile_lstmcell_pa_t_kernel(tc, x, me_output, W_memi, W_memh, W_memt, mem_bias
             cols = ROW_TILES[j] * P
             codes = work.tile([P, cols], U32, name="%sc%d" % (nm, j), tag=nm + "c", bufs=bufs, align_bytes=64)
             scales = work.tile([P, cols], U8, name="%ss%d" % (nm, j), tag=nm + "s", bufs=bufs, align_bytes=64)
-            nc.vector.quantize_mx(out=codes[:].bitcast(FP8X4), scales=scales[:], in_=src[:])
+            nc.vector.quantize_mx(out=codes[:].bitcast(FP8X4), scales=scales[:], in_=src)
             st[(nm, j)] = (codes, scales)
+
+        def quant_xe(j):
+            quant(st[("gx", j)][:], "x", j, 2)
+            quant(st[("ge", j)][:], "e", j, 2)
+            st[("x", j)] = tuple(t[:] for t in st[("x", j)])
+            st[("e", j)] = tuple(t[:] for t in st[("e", j)])
 
         def stage1(j):
             n = ROW_TILES[j] * P
             per_bank = 512 // n
             xc, xs = st[("x", j)]
             ec, es = st[("e", j)]
+            wic, wis = st["wi"]
+            whc, whs = st["wh"]
             bank = None
             for m in range(4):
                 cols = slice(m * P, (m + 1) * P)
@@ -189,17 +214,17 @@ def tile_lstmcell_pa_t_kernel(tc, x, me_output, W_memi, W_memh, W_memt, mem_bias
                 acc = bank[:, (m % per_bank) * n:(m % per_bank + 1) * n]
                 nc.tensor.matmul_mx(
                     out=acc, lhsT=wic[:, cols].bitcast(FP8X4), lhsT_scale=wis[:, cols],
-                    rhs=xc[:].bitcast(FP8X4), rhs_scale=xs[:], start=True, stop=False,
+                    rhs=xc.bitcast(FP8X4), rhs_scale=xs, start=True, stop=False,
                 )
                 nc.tensor.matmul_mx(
                     out=acc, lhsT=whc[:, cols].bitcast(FP8X4), lhsT_scale=whs[:, cols],
-                    rhs=ec[:].bitcast(FP8X4), rhs_scale=es[:], start=False, stop=True,
+                    rhs=ec.bitcast(FP8X4), rhs_scale=es, start=False, stop=True,
                 )
                 st[("M", j, m)] = acc
 
         def sigmoid(j):
             n = ROW_TILES[j] * P
-            sig = work.tile([P, 4 * n], F32, name="sig%d" % j, tag="sig")
+            sig = work.tile([P, 4 * n], F32, name="sig%d" % j, tag="sig", bufs=2)
             for m in range(4):
                 nc.scalar.activation(
                     out=sig[:, m * n:(m + 1) * n], in_=st[("M", j, m)],
@@ -207,33 +232,98 @@ def tile_lstmcell_pa_t_kernel(tc, x, me_output, W_memi, W_memh, W_memt, mem_bias
                 )
             st[("sig", j)] = sig
 
-        def mult(j):
-            n = ROW_TILES[j] * P
-            gg = work.tile([P, 4 * n], BF16, name="gg%d" % j, tag="gg", align_bytes=64)
-            nv = n - gpsimd_cols(j)
-            planes = st[("sig", j)][:].rearrange("p (t c) -> p t c", t=4)
-            ge = st[("ge", j)]
-            nc.vector.tensor_tensor(
-                out=gg[:, :4 * nv].rearrange("p (c i t) -> p c t i", i=4, t=4),
-                in0=planes[:, :, :nv].rearrange("p t (c i) -> p c t i", i=4),
-                in1=ge[:, :4 * nv].rearrange("p (c i t) -> p c t i", i=4, t=4),
-                op=ALU.mult,
-            )
-            if nv < n:
-                nc.gpsimd.tensor_tensor(
-                    out=gg[:, 4 * nv:].rearrange("p (c t) -> p c t", t=4),
-                    in0=planes[:, :, nv:].rearrange("p t c -> p c t"),
-                    in1=ge[:, 4 * nv:].rearrange("p (c t) -> p c t", t=4),
+        def product(engine, j, a, b):
+            planes = st[("sig", j)][:].rearrange("p (t c) -> p t c", t=4)[:, :, a:b]
+            if engine == "v":
+                nc.vector.tensor_tensor(
+                    out=st[("gg", j)][:, 4 * a:4 * b].rearrange("p (c i t) -> p c t i", i=4, t=4),
+                    in0=planes.rearrange("p t (c i) -> p c t i", i=4),
+                    in1=st[("ge", j)][:, 4 * a:4 * b].rearrange("p (c i t) -> p c t i", i=4, t=4),
                     op=ALU.mult,
                 )
-            st[("gg", j)] = gg
+            else:
+                nc.gpsimd.tensor_tensor(
+                    out=st[("gg", j)][:, 4 * a:4 * b].rearrange("p (c t) -> p c t", t=4),
+                    in0=planes.rearrange("p t c -> p c t"),
+                    in1=st[("ge", j)][:, 4 * a:4 * b].rearrange("p (c t) -> p c t", t=4),
+                    op=ALU.mult,
+                )
+
+        def product_psum(j, a, b):
+            nr = ROW_TILES[j]
+            h, m = halves(j)[-1]
+            c0 = a - 2 * h * P
+            bank = st[("T", "en", j, h)][:, :m * 256].bitcast(BF16).rearrange("p (u c e) -> p u c e", u=2, e=2)
+            planes = st[("sig", j)][:].rearrange("p (u e c) -> p u e c", u=2, e=2)
+            gg = st[("gg", j)][:, 4 * a:4 * b]
+            nc.vector.tensor_tensor(
+                out=gg.rearrange("p (c i u e) -> p c u e i", i=4, u=2, e=2),
+                in0=planes[:, :, :, a:b].rearrange("p u e (c i) -> p c u e i", i=4),
+                in1=bank[:, :, c0:c0 + b - a, :].rearrange("p u (c i) e -> p c u e i", i=4),
+                op=ALU.mult,
+            )
+
+        def splits(j):
+            n = ROW_TILES[j] * P
+            p0 = n - psum_cols(j)
+            return p0 - gpsimd_cols(j), p0, n
+
+        def alloc_gg(j):
+            n = ROW_TILES[j] * P
+            st[("gg", j)] = work.tile([P, 4 * n], BF16, name="gg%d" % j, tag="gg", bufs=2, align_bytes=64)
+
+        def mult_first(j):
+            g0, p0, n = splits(j)
+            if p0 < n:
+                product_psum(j, p0, n)
+            if g0 < p0:
+                product("g", j, g0, p0)
+
+        def mult_rest(j):
+            g0 = splits(j)[0]
+            if g0:
+                product("v", j, 0, g0)
+
+        def finish(j):
+            nr = ROW_TILES[j]
+            for r in range(nr):
+                gg = work.tile([P, 512], BF16, name="gl%d" % r, tag="gl", align_bytes=64)
+                a, b = r * P, (r + 1) * P
+                nc.vector.tensor_tensor(
+                    out=gg[:].rearrange("p (c i t) -> p c t i", i=4, t=4),
+                    in0=st[("sig", j)][:].rearrange("p (t c) -> p t c", t=4)[:, :, a:b].rearrange("p t (c i) -> p c t i", i=4),
+                    in1=st[("ge", j)][:, 4 * a:4 * b].rearrange("p (c i t) -> p c t i", i=4, t=4),
+                    op=ALU.mult,
+                )
+                st[("gl", r)] = gg
+            for r in range(nr):
+                codes = work.tile([P, P], U32, name="glc%d" % r, tag="glc", align_bytes=64)
+                scales = work.tile([P, P], U8, name="gls%d" % r, tag="gls", align_bytes=64)
+                nc.vector.quantize_mx(out=codes[:].bitcast(FP8X4), scales=scales[:], in_=st[("gl", r)][:])
+                st[("glq", r)] = (codes, scales)
+
+        def finish2(j):
+            nr = ROW_TILES[j]
+            wtc, wts = st["wt"]
+            view = out[ROW0[j]:ROW0[j] + nr * P, :].rearrange("(p r) h -> p r h", r=nr)
+            for r in range(nr):
+                bank = new_bank()
+                gc, gs = st[("glq", r)]
+                nc.tensor.matmul_mx(
+                    out=bank[:, :H], lhsT=gc[:].bitcast(FP8X4), lhsT_scale=gs[:],
+                    rhs=wtc[:].bitcast(FP8X4), rhs_scale=wts[:], start=True, stop=True,
+                )
+                osb = work.tile([P, H], F32, name="ol%d" % r, tag="ol")
+                copy = nc.scalar.copy if r == 0 else nc.vector.tensor_copy
+                copy(out=osb[:], in_=bank[:, :H])
+                nc.sync.dma_start(out=view[:, r, :], in_=osb[:])
 
         def stage2(j):
             gc, gs = st[("g", j)]
             wtc, wts = st["wt"]
-            for h in range(ROW_TILES[j] // 2):
+            for h, m in halves(j):
                 bank = new_bank()
-                for rr in range(2):
+                for rr in range(m):
                     cols = slice((2 * h + rr) * P, (2 * h + rr + 1) * P)
                     nc.tensor.matmul_mx(
                         out=bank[:, rr * H:(rr + 1) * H],
@@ -245,22 +335,28 @@ def tile_lstmcell_pa_t_kernel(tc, x, me_output, W_memi, W_memh, W_memt, mem_bias
         def oexit_store(j):
             nr = ROW_TILES[j]
             osb = work.tile([P, nr * H], F32, name="osb%d" % j, tag="osb", bufs=3)
-            for h in range(nr // 2):
-                nc.scalar.copy(out=osb[:, h * 512:(h + 1) * 512], in_=st[("O", j, h)][:])
+            for h, m in halves(j):
+                copy = nc.vector.tensor_copy if False else nc.scalar.copy
+                copy(out=osb[:, h * 512:h * 512 + m * H], in_=st[("O", j, h)][:, :m * H])
             nc.sync.dma_start(
                 out=out[ROW0[j]:ROW0[j] + nr * P, :].rearrange("(p r) h -> p (r h)", r=nr), in_=osb[:]
             )
 
+        prep_gate()
         for s in range(-2, NB + S2_LAG):
             while loaded[0] < NB and loaded[0] <= s + LOOKAHEAD:
                 load(loaded[0])
                 loaded[0] += 1
             if s + 2 < NB:
                 transposes(s + 2)
-            if 0 <= s + 3 < NB:
-                reorder(s + 3)
-            if 0 <= s < NB:
-                mult(s)
+            if 0 <= s + REORDER_LEAD < NB:
+                reorder(s + REORDER_LEAD)
+            if s == NB - 1:
+                finish(s)
+            if 0 <= s < NB - 1:
+                alloc_gg(s)
+                mult_rest(s)
+                mult_first(s)
             if s + 2 < NB:
                 exits(s + 2)
             if s == 0:
@@ -269,12 +365,13 @@ def tile_lstmcell_pa_t_kernel(tc, x, me_output, W_memi, W_memh, W_memt, mem_bias
                 stage1(s + 1)
                 sigmoid(s + 1)
             if s + 2 < NB:
-                quant(st[("gx", s + 2)], "x", s + 2, 2)
-                quant(st[("ge", s + 2)], "e", s + 2, 2)
-            if 0 <= s < NB:
-                quant(st[("gg", s)], "g", s, 2 + S2_LAG)
+                quant_xe(s + 2)
+            if 0 <= s < NB - 1:
+                quant(st[("gg", s)][:], "g", s, 2 + S2_LAG)
             if s == -1:
                 prep_wt()
-            if 0 <= s - S2_LAG < NB:
+            if 0 <= s - S2_LAG < NB - 1:
                 stage2(s - S2_LAG)
                 oexit_store(s - S2_LAG)
+            if s == NB - 1:
+                finish2(s)

@@ -151,8 +151,8 @@ def tile_lstmcell_pa_t_kernel(tc, x, me_output, W_memi, W_memh, W_memt, mem_bias
         def halves(j):
             return [(h, min(2, ROW_TILES[j] - 2 * h)) for h in range((ROW_TILES[j] + 1) // 2)]
 
-        def transposes(j):
-            for key in ("xn", "en"):
+        def transposes(j, key):
+            if True:
                 words = st[(key, j)][:].bitcast(F32)
                 for h, m in halves(j):
                     if HELD_BANKS and key == "en" and h == len(halves(j)) - 1:
@@ -173,12 +173,15 @@ def tile_lstmcell_pa_t_kernel(tc, x, me_output, W_memi, W_memh, W_memt, mem_bias
             st[("gx", j)] = work.tile([P, nr * 512], BF16, name="gx%d" % j, tag="gx", bufs=2, align_bytes=64)
             st[("ge", j)] = work.tile([P, nr * 512], BF16, name="ge%d" % j, tag="ge", bufs=3, align_bytes=64)
 
-        def exits(j):
-            exit_tiles(j)
+        def exits(j, which):
+            if which == "xn":
+                exit_tiles(j)
             gx, ge = st[("gx", j)], st[("ge", j)]
             plan = [("xn", gx, h, m) for h, m in halves(j)] + [("en", ge, h, m) for h, m in halves(j)]
             n_vec = vector_exits(j)
             for i, (key, dst, h, m) in enumerate(plan):
+                if key != which:
+                    continue
                 src = st[("T", key, j, h)][:, :m * 256].rearrange("q (u c) -> q c u", u=2)
                 d = dst[:].bitcast(F32)[:, h * 512:h * 512 + m * 256].rearrange("q (c u) -> q c u", u=2)
                 if i >= len(plan) - n_vec:
@@ -199,7 +202,7 @@ def tile_lstmcell_pa_t_kernel(tc, x, me_output, W_memi, W_memh, W_memt, mem_bias
             st[("x", j)] = tuple(t[:] for t in st[("x", j)])
             st[("e", j)] = tuple(t[:] for t in st[("e", j)])
 
-        def stage1(j):
+        def stage1(j, planes):
             n = ROW_TILES[j] * P
             per_bank = 512 // n
             xc, xs = st[("x", j)]
@@ -207,9 +210,9 @@ def tile_lstmcell_pa_t_kernel(tc, x, me_output, W_memi, W_memh, W_memt, mem_bias
             wic, wis = st["wi"]
             whc, whs = st["wh"]
             bank = None
-            for m in range(4):
+            for m in planes:
                 cols = slice(m * P, (m + 1) * P)
-                if m % per_bank == 0:
+                if m % per_bank == 0 or bank is None:
                     bank = new_bank()
                 acc = bank[:, (m % per_bank) * n:(m % per_bank + 1) * n]
                 nc.tensor.matmul_mx(
@@ -222,15 +225,16 @@ def tile_lstmcell_pa_t_kernel(tc, x, me_output, W_memi, W_memh, W_memt, mem_bias
                 )
                 st[("M", j, m)] = acc
 
-        def sigmoid(j):
+        def sigmoid(j, ms):
             n = ROW_TILES[j] * P
-            sig = work.tile([P, 4 * n], F32, name="sig%d" % j, tag="sig", bufs=2)
-            for m in range(4):
+            if 0 in ms:
+                st[("sig", j)] = work.tile([P, 4 * n], F32, name="sig%d" % j, tag="sig", bufs=2)
+            sig = st[("sig", j)]
+            for m in ms:
                 nc.scalar.activation(
                     out=sig[:, m * n:(m + 1) * n], in_=st[("M", j, m)],
                     func=ACT.Sigmoid, bias=bias_f[:, m:m + 1], scale=1.0,
                 )
-            st[("sig", j)] = sig
 
         def product(engine, j, a, b):
             planes = st[("sig", j)][:].rearrange("p (t c) -> p t c", t=4)[:, :, a:b]
@@ -348,7 +352,7 @@ def tile_lstmcell_pa_t_kernel(tc, x, me_output, W_memi, W_memh, W_memt, mem_bias
                 load(loaded[0])
                 loaded[0] += 1
             if s + 2 < NB:
-                transposes(s + 2)
+                transposes(s + 2, "xn")
             if 0 <= s + REORDER_LEAD < NB:
                 reorder(s + REORDER_LEAD)
             if s == NB - 1:
@@ -358,12 +362,18 @@ def tile_lstmcell_pa_t_kernel(tc, x, me_output, W_memi, W_memh, W_memt, mem_bias
                 mult_rest(s)
                 mult_first(s)
             if s + 2 < NB:
-                exits(s + 2)
+                exits(s + 2, "xn")
             if s == 0:
                 quant_wt()
             if 0 <= s + 1 < NB:
-                stage1(s + 1)
-                sigmoid(s + 1)
+                stage1(s + 1, (0, 1))
+                sigmoid(s + 1, (0, 1))
+            if s + 2 < NB:
+                transposes(s + 2, "en")
+                exits(s + 2, "en")
+            if 0 <= s + 1 < NB:
+                stage1(s + 1, (2, 3))
+                sigmoid(s + 1, (2, 3))
             if s + 2 < NB:
                 quant_xe(s + 2)
             if 0 <= s < NB - 1:

@@ -15,7 +15,7 @@ B, I, OH, H = 8192, 512, 512, 256
 FLOPS = 2 * B * (I * OH + OH * OH + OH * H)
 
 P = 128
-ROW_TILES = [2, 2] + [4] * 14 + [2, 2]
+ROW_TILES = [4]*15+[2,2]
 NB = len(ROW_TILES)
 ROW0 = [P * sum(ROW_TILES[:j]) for j in range(NB)]
 assert P * sum(ROW_TILES) == B
@@ -29,7 +29,7 @@ REORDER_LEAD = 3
 
 def reorder_plan(j):
     nr = ROW_TILES[j]
-    return [("xn", 0, 1)] if nr == 4 and j >= 4 else []
+    return [("xn", 0, 1)] if nr == 4 and j >= 3 else []
 
 
 def vector_exits(j):

@@ -29,12 +29,12 @@ REORDER_LEAD = 3
 
 def reorder_plan(j):
     nr = ROW_TILES[j]
-    return [("xn", 0, 1)] if nr == 4 and j >= 3 else []
+    return [("xn", 0, 1)] if nr == 4 and j >= 4 else []
 
 
 def vector_exits(j):
     nr = ROW_TILES[j]
-    return (0 if j < 2 else 1 if nr < 4 else 2 if j % 3 == 1 else 1)
+    return (0 if j in (0, NB - 1) else 1 if nr < 4 else 2 if j % 3 == 1 else 1)
 
 
 def psum_cols(j):
@@ -44,7 +44,7 @@ def psum_cols(j):
 
 def gpsimd_cols(j):
     nr = ROW_TILES[j]
-    return (48 * vector_exits(j + 2) if nr == 4 and j + 2 < NB else 0)
+    return (48 * max(1, vector_exits(j + 2)) if nr == 4 and j + 2 < NB else 0)
 
 
 def tile_lstmcell_pa_t_kernel(tc, x, me_output, W_memi, W_memh, W_memt, mem_bias, out):
@@ -227,7 +227,7 @@ def tile_lstmcell_pa_t_kernel(tc, x, me_output, W_memi, W_memh, W_memt, mem_bias
 
         def sigmoid(j, ms):
             n = ROW_TILES[j] * P
-            if 0 in ms:
+            if ("sig", j) not in st:
                 st[("sig", j)] = work.tile([P, 4 * n], F32, name="sig%d" % j, tag="sig", bufs=2)
             sig = st[("sig", j)]
             for m in ms:
@@ -365,15 +365,16 @@ def tile_lstmcell_pa_t_kernel(tc, x, me_output, W_memi, W_memh, W_memt, mem_bias
                 exits(s + 2, "xn")
             if s == 0:
                 quant_wt()
+            early = 0 if s < 0 else 2
             if 0 <= s + 1 < NB:
-                stage1(s + 1, (0, 1))
-                sigmoid(s + 1, (0, 1))
+                stage1(s + 1, range(early))
+                sigmoid(s + 1, range(early))
             if s + 2 < NB:
                 transposes(s + 2, "en")
                 exits(s + 2, "en")
             if 0 <= s + 1 < NB:
-                stage1(s + 1, (2, 3))
-                sigmoid(s + 1, (2, 3))
+                stage1(s + 1, range(early, 4))
+                sigmoid(s + 1, range(early, 4))
             if s + 2 < NB:
                 quant_xe(s + 2)
             if 0 <= s < NB - 1:

from contextlib import ExitStack

import concourse.mybir as mybir
from concourse.masks import make_identity

F32 = mybir.dt.float32
BF16 = mybir.dt.bfloat16
U32 = mybir.dt.uint32
U8 = mybir.dt.uint8
FP8X4 = mybir.dt.float8_e4m3fn_x4
ACT = mybir.ActivationFunctionType
ALU = mybir.AluOpType

B, I, OH, H = 8192, 512, 512, 256
FLOPS = 2 * B * (I * OH + OH * OH + OH * H)

P = 128
ROW_TILES = [4]*15+[2,2]
NB = len(ROW_TILES)
ROW0 = [P * sum(ROW_TILES[:j]) for j in range(NB)]
assert P * sum(ROW_TILES) == B
LOOKAHEAD = 6
NAT_BUFS = 6
S2_LAG = 1
RING_BANKS = 8
HELD_BANKS = 0
REORDER_LEAD = 3


def reorder_plan(j):
    nr = ROW_TILES[j]
    return [("xn", 0, 1)] if nr == 4 and j >= 4 else []


def vector_exits(j):
    nr = ROW_TILES[j]
    return (0 if j in (0, NB - 1) else 1 if nr < 4 else 2 if j % 3 == 1 else 1)


def psum_cols(j):
    nr = ROW_TILES[j]
    return 0


def gpsimd_cols(j):
    nr = ROW_TILES[j]
    return (48 * max(1, vector_exits(j + 2)) if nr == 4 and j + 2 < NB else 0)


def tile_lstmcell_pa_t_kernel(tc, x, me_output, W_memi, W_memh, W_memt, mem_bias, out):
    nc = tc.nc
    with ExitStack() as ctx:
        consts = ctx.enter_context(tc.tile_pool(name="consts", bufs=1))
        nat = ctx.enter_context(tc.tile_pool(name="nat", bufs=NAT_BUFS))
        work = ctx.enter_context(tc.tile_pool(name="work", bufs=2))
        psum = ctx.enter_context(tc.psum_pool(name="psum", bufs=1))
        ctx.enter_context(tc.manual_schedule())

        counter = [0]

        def new_bank():
            n = counter[0]
            counter[0] = n + 1
            return psum.tile([P, 512], F32, name="ps%d" % n, tag="bank%d" % (n % RING_BANKS))

        st = {}

        warm = consts.tile([P, 1], F32, name="warm")
        nc.vector.memset(warm[:], 0.0)
        nc.scalar.activation(out=warm[:], in_=warm[:], func=ACT.Sigmoid)

        ident = consts.tile([P, P], F32, name="ident")
        make_identity(nc, ident[:])

        bias_raw = consts.tile([P, 4], BF16, name="bias_raw")
        with nc.allow_non_contiguous_dma(reason="512 bias values, four to a partition"):
            nc.scalar.dma_start(out=bias_raw[:], in_=mem_bias.rearrange("(p t) -> p t", t=4))

        def load_w(w, cols, nm):
            raw = consts.tile([P, 4 * cols], BF16, name=nm + "_raw")
            nc.sync.dma_start(out=raw[:], in_=w.rearrange("(p j) c -> p (j c)", j=4))
            return raw

        def load(j):
            nr = ROW_TILES[j]
            rows = slice(ROW0[j], ROW0[j] + nr * P)
            xn = nat.tile([P, nr * I], BF16, name="xn%d" % j, tag="xn")
            nc.sync.dma_start(out=xn[:], in_=x[rows, :].rearrange("(p r) k -> p (r k)", r=nr))
            en = nat.tile([P, nr * OH], BF16, name="en%d" % j, tag="en")
            nc.sync.dma_start(out=en[:], in_=me_output[rows, :].rearrange("(p r) k -> p (r k)", r=nr))
            st[("xn", j)] = xn
            st[("en", j)] = en

        wi_raw = load_w(W_memi, OH, "wi")
        wh_raw = load_w(W_memh, OH, "wh")
        load(0)
        load(1)
        wt_raw = load_w(W_memt, H, "wt")
        load(2)
        load(3)
        loaded = [4]

        def regroup_gate_w(raw, nm, engines):
            grp = consts.tile([P, 4 * OH], BF16, name=nm + "_grp", align_bytes=64)
            src = raw[:].rearrange("p (t q m) -> p m q t", t=4, m=4)
            for m in range(4):
                dst = grp[:, m * 512:(m + 1) * 512].rearrange("p (q t) -> p q t", t=4)
                if engines[m] == "v":
                    nc.vector.tensor_copy(out=dst, in_=src[:, m])
                else:
                    nc.scalar.copy(out=dst, in_=src[:, m])
            return grp

        def quant_w(grp, cols, nm):
            codes = consts.tile([P, cols], U32, name=nm + "_codes", align_bytes=64)
            scales = consts.tile([P, cols], U8, name=nm + "_scales", align_bytes=64)
            nc.vector.quantize_mx(out=codes[:].bitcast(FP8X4), scales=scales[:], in_=grp[:])
            return codes, scales

        bias_f = consts.tile([P, 4], F32, name="bias_f")

        def prep_gate():
            wi_grp = regroup_gate_w(wi_raw, "wi", "vvvs")
            st["wi"] = quant_w(wi_grp, OH, "wi")
            wh_grp = regroup_gate_w(wh_raw, "wh", "ssvv")
            st["wh"] = quant_w(wh_grp, OH, "wh")
            nc.vector.tensor_copy(out=bias_f[:], in_=bias_raw[:])

        def prep_wt():
            grp = consts.tile([P, 4 * H], BF16, name="wt_grp", align_bytes=64)
            nc.vector.tensor_copy(
                out=grp[:].rearrange("p (h t) -> p h t", t=4),
                in_=wt_raw[:].rearrange("p (t h) -> p h t", t=4),
            )
            st["wt_grp"] = grp

        def quant_wt():
            st["wt"] = quant_w(st["wt_grp"], H, "wt")

        def reorder(j):
            for key, r0, m in reorder_plan(j):
                dst = work.tile([P, m * 256], F32, name="%sw%d" % (key, j), tag=key + "w")
                nc.vector.tensor_copy(
                    out=dst[:].rearrange("p (r u q) -> p u r q", u=2, r=m),
                    in_=st[(key, j)][:].bitcast(F32)[:, r0 * 256:(r0 + m) * 256].rearrange("p (r q u) -> p u r q", u=2, r=m),
                )
                for r in range(m):
                    for u in range(2):
                        st[("W", key, j, r0 + r, u)] = dst[:, (2 * r + u) * P:(2 * r + u + 1) * P]

        def halves(j):
            return [(h, min(2, ROW_TILES[j] - 2 * h)) for h in range((ROW_TILES[j] + 1) // 2)]

        def transposes(j, key):
            if True:
                words = st[(key, j)][:].bitcast(F32)
                for h, m in halves(j):
                    if HELD_BANKS and key == "en" and h == len(halves(j)) - 1:
                        bank = psum.tile([P, 512], F32, name="held%d" % j, tag="held", bufs=HELD_BANKS)
                    else:
                        bank = new_bank()
                    for rr in range(m):
                        for u in range(2):
                            c0 = (2 * h + rr) * 256 + u
                            src = st.get(("W", key, j, 2 * h + rr, u))
                            if src is None:
                                src = words[:, c0:c0 + 255:2]
                            nc.tensor.transpose(bank[:, (u * m + rr) * P:(u * m + rr + 1) * P], src, ident[:])
                    st[("T", key, j, h)] = bank

        def exit_tiles(j):
            nr = ROW_TILES[j]
            st[("gx", j)] = work.tile([P, nr * 512], BF16, name="gx%d" % j, tag="gx", bufs=2, align_bytes=64)
            st[("ge", j)] = work.tile([P, nr * 512], BF16, name="ge%d" % j, tag="ge", bufs=3, align_bytes=64)

        def exits(j, which):
            if which == "xn":
                exit_tiles(j)
            gx, ge = st[("gx", j)], st[("ge", j)]
            plan = [("xn", gx, h, m) for h, m in halves(j)] + [("en", ge, h, m) for h, m in halves(j)]
            n_vec = vector_exits(j)
            for i, (key, dst, h, m) in enumerate(plan):
                if key != which:
                    continue
                src = st[("T", key, j, h)][:, :m * 256].rearrange("q (u c) -> q c u", u=2)
                d = dst[:].bitcast(F32)[:, h * 512:h * 512 + m * 256].rearrange("q (c u) -> q c u", u=2)
                if i >= len(plan) - n_vec:
                    nc.vector.tensor_copy(out=d, in_=src)
                else:
                    nc.scalar.copy(out=d, in_=src)

        def quant(src, nm, j, bufs):
            cols = ROW_TILES[j] * P
            codes = work.tile([P, cols], U32, name="%sc%d" % (nm, j), tag=nm + "c", bufs=bufs, align_bytes=64)
            scales = work.tile([P, cols], U8, name="%ss%d" % (nm, j), tag=nm + "s", bufs=bufs, align_bytes=64)
            nc.vector.quantize_mx(out=codes[:].bitcast(FP8X4), scales=scales[:], in_=src)
            st[(nm, j)] = (codes, scales)

        def quant_xe(j):
            quant(st[("gx", j)][:], "x", j, 2)
            quant(st[("ge", j)][:], "e", j, 2)
            st[("x", j)] = tuple(t[:] for t in st[("x", j)])
            st[("e", j)] = tuple(t[:] for t in st[("e", j)])

        def stage1(j, planes):
            n = ROW_TILES[j] * P
            per_bank = 512 // n
            xc, xs = st[("x", j)]
            ec, es = st[("e", j)]
            wic, wis = st["wi"]
            whc, whs = st["wh"]
            bank = None
            for m in planes:
                cols = slice(m * P, (m + 1) * P)
                if m % per_bank == 0 or bank is None:
                    bank = new_bank()
                acc = bank[:, (m % per_bank) * n:(m % per_bank + 1) * n]
                nc.tensor.matmul_mx(
                    out=acc, lhsT=wic[:, cols].bitcast(FP8X4), lhsT_scale=wis[:, cols],
                    rhs=xc.bitcast(FP8X4), rhs_scale=xs, start=True, stop=False,
                )
                nc.tensor.matmul_mx(
                    out=acc, lhsT=whc[:, cols].bitcast(FP8X4), lhsT_scale=whs[:, cols],
                    rhs=ec.bitcast(FP8X4), rhs_scale=es, start=False, stop=True,
                )
                st[("M", j, m)] = acc

        def sigmoid(j, ms):
            n = ROW_TILES[j] * P
            if ("sig", j) not in st:
                st[("sig", j)] = work.tile([P, 4 * n], F32, name="sig%d" % j, tag="sig", bufs=2)
            sig = st[("sig", j)]
            for m in ms:
                nc.scalar.activation(
                    out=sig[:, m * n:(m + 1) * n], in_=st[("M", j, m)],
                    func=ACT.Sigmoid, bias=bias_f[:, m:m + 1], scale=1.0,
                )

        def product(engine, j, a, b):
            planes = st[("sig", j)][:].rearrange("p (t c) -> p t c", t=4)[:, :, a:b]
            if engine == "v":
                nc.vector.tensor_tensor(
                    out=st[("gg", j)][:, 4 * a:4 * b].rearrange("p (c i t) -> p c t i", i=4, t=4),
                    in0=planes.rearrange("p t (c i) -> p c t i", i=4),
                    in1=st[("ge", j)][:, 4 * a:4 * b].rearrange("p (c i t) -> p c t i", i=4, t=4),
                    op=ALU.mult,
                )
            else:
                nc.gpsimd.tensor_tensor(
                    out=st[("gg", j)][:, 4 * a:4 * b].rearrange("p (c t) -> p c t", t=4),
                    in0=planes.rearrange("p t c -> p c t"),
                    in1=st[("ge", j)][:, 4 * a:4 * b].rearrange("p (c t) -> p c t", t=4),
                    op=ALU.mult,
                )

        def product_psum(j, a, b):
            nr = ROW_TILES[j]
            h, m = halves(j)[-1]
            c0 = a - 2 * h * P
            bank = st[("T", "en", j, h)][:, :m * 256].bitcast(BF16).rearrange("p (u c e) -> p u c e", u=2, e=2)
            planes = st[("sig", j)][:].rearrange("p (u e c) -> p u e c", u=2, e=2)
            gg = st[("gg", j)][:, 4 * a:4 * b]
            nc.vector.tensor_tensor(
                out=gg.rearrange("p (c i u e) -> p c u e i", i=4, u=2, e=2),
                in0=planes[:, :, :, a:b].rearrange("p u e (c i) -> p c u e i", i=4),
                in1=bank[:, :, c0:c0 + b - a, :].rearrange("p u (c i) e -> p c u e i", i=4),
                op=ALU.mult,
            )

        def splits(j):
            n = ROW_TILES[j] * P
            p0 = n - psum_cols(j)
            return p0 - gpsimd_cols(j), p0, n

        def alloc_gg(j):
            n = ROW_TILES[j] * P
            st[("gg", j)] = work.tile([P, 4 * n], BF16, name="gg%d" % j, tag="gg", bufs=2, align_bytes=64)

        def mult_first(j):
            g0, p0, n = splits(j)
            if p0 < n:
                product_psum(j, p0, n)
            if g0 < p0:
                product("g", j, g0, p0)

        def mult_rest(j):
            g0 = splits(j)[0]
            if g0:
                product("v", j, 0, g0)

        def finish(j):
            nr = ROW_TILES[j]
            for r in range(nr):
                gg = work.tile([P, 512], BF16, name="gl%d" % r, tag="gl", align_bytes=64)
                a, b = r * P, (r + 1) * P
                nc.vector.tensor_tensor(
                    out=gg[:].rearrange("p (c i t) -> p c t i", i=4, t=4),
                    in0=st[("sig", j)][:].rearrange("p (t c) -> p t c", t=4)[:, :, a:b].rearrange("p t (c i) -> p c t i", i=4),
                    in1=st[("ge", j)][:, 4 * a:4 * b].rearrange("p (c i t) -> p c t i", i=4, t=4),
                    op=ALU.mult,
                )
                st[("gl", r)] = gg
            for r in range(nr):
                codes = work.tile([P, P], U32, name="glc%d" % r, tag="glc", align_bytes=64)
                scales = work.tile([P, P], U8, name="gls%d" % r, tag="gls", align_bytes=64)
                nc.vector.quantize_mx(out=codes[:].bitcast(FP8X4), scales=scales[:], in_=st[("gl", r)][:])
                st[("glq", r)] = (codes, scales)

        def finish2(j):
            nr = ROW_TILES[j]
            wtc, wts = st["wt"]
            view = out[ROW0[j]:ROW0[j] + nr * P, :].rearrange("(p r) h -> p r h", r=nr)
            for r in range(nr):
                bank = new_bank()
                gc, gs = st[("glq", r)]
                nc.tensor.matmul_mx(
                    out=bank[:, :H], lhsT=gc[:].bitcast(FP8X4), lhsT_scale=gs[:],
                    rhs=wtc[:].bitcast(FP8X4), rhs_scale=wts[:], start=True, stop=True,
                )
                osb = work.tile([P, H], F32, name="ol%d" % r, tag="ol")
                copy = nc.scalar.copy if r == 0 else nc.vector.tensor_copy
                copy(out=osb[:], in_=bank[:, :H])
                nc.sync.dma_start(out=view[:, r, :], in_=osb[:])

        def stage2(j):
            gc, gs = st[("g", j)]
            wtc, wts = st["wt"]
            for h, m in halves(j):
                bank = new_bank()
                for rr in range(m):
                    cols = slice((2 * h + rr) * P, (2 * h + rr + 1) * P)
                    nc.tensor.matmul_mx(
                        out=bank[:, rr * H:(rr + 1) * H],
                        lhsT=gc[:, cols].bitcast(FP8X4), lhsT_scale=gs[:, cols],
                        rhs=wtc[:].bitcast(FP8X4), rhs_scale=wts[:], start=True, stop=True,
                    )
                st[("O", j, h)] = bank

        def oexit_store(j):
            nr = ROW_TILES[j]
            osb = work.tile([P, nr * H], F32, name="osb%d" % j, tag="osb", bufs=3)
            for h, m in halves(j):
                copy = nc.vector.tensor_copy if False else nc.scalar.copy
                copy(out=osb[:, h * 512:h * 512 + m * H], in_=st[("O", j, h)][:, :m * H])
            nc.sync.dma_start(
                out=out[ROW0[j]:ROW0[j] + nr * P, :].rearrange("(p r) h -> p (r h)", r=nr), in_=osb[:]
            )

        prep_gate()
        for s in range(-2, NB + S2_LAG):
            while loaded[0] < NB and loaded[0] <= s + LOOKAHEAD:
                load(loaded[0])
                loaded[0] += 1
            if s + 2 < NB:
                transposes(s + 2, "xn")
            if 0 <= s + REORDER_LEAD < NB:
                reorder(s + REORDER_LEAD)
            if s == NB - 1:
                finish(s)
            if 0 <= s < NB - 1:
                alloc_gg(s)
                mult_rest(s)
                mult_first(s)
            if s + 2 < NB:
                exits(s + 2, "xn")
            if s == 0:
                quant_wt()
            early = 0 if s < 0 else 2
            if 0 <= s + 1 < NB:
                stage1(s + 1, range(early))
                sigmoid(s + 1, range(early))
            if s + 2 < NB:
                transposes(s + 2, "en")
                exits(s + 2, "en")
            if 0 <= s + 1 < NB:
                stage1(s + 1, range(early, 4))
                sigmoid(s + 1, range(early, 4))
            if s + 2 < NB:
                quant_xe(s + 2)
            if 0 <= s < NB - 1:
                quant(st[("gg", s)][:], "g", s, 2 + S2_LAG)
            if s == -1:
                prep_wt()
            if 0 <= s - S2_LAG < NB - 1:
                stage2(s - S2_LAG)
                oexit_store(s - S2_LAG)
            if s == NB - 1:
                finish2(s)
